import numpy as np
import ml_dtypes

BF16 = ml_dtypes.bfloat16


def bf(x):
    return np.asarray(x, np.float32).astype(BF16)


def f32(x):
    return np.asarray(x, np.float32)


def f64(x):
    return np.asarray(x).astype(np.float64)


def striped(idx):
    return np.tile(idx.reshape(-1, 16).T, (8, 1))


H, D, HALF, C, S, N, T = 8, 128, 64, 1024, 256, 128, 128
SCALE = D ** -0.5


def rope(u, cos, sin):
    u3 = u.reshape(H, D, -1)
    rot = np.concatenate([-u3[:, HALF:], u3[:, :HALF]], axis=1)
    c2 = np.concatenate([cos, cos], axis=0)[None]
    s2 = np.concatenate([sin, sin], axis=0)[None]
    return u3 * c2 + rot * s2


def setup_inputs():
    theta = np.random.uniform(0.0, 2.0 * np.pi, (HALF, N))
    return {"kstore": bf(np.random.standard_normal((C, S))), "x": bf(np.random.standard_normal((C, T))), "v": bf(2.0 * np.random.standard_normal((N, C))), "cos": bf(np.cos(theta)), "sin": bf(np.sin(theta)), "mask": f32(0.5 * np.random.standard_normal((T, N))), "offs": striped(np.random.permutation(S)[:N])}


def reference(kstore, x, v, cos, sin, mask, offs):
    idx = offs[:16].T.reshape(-1)
    k = rope(f64(kstore)[:, idx], f64(cos), f64(sin))
    q = rope(f64(x), f64(cos), f64(sin))
    sc = np.einsum("hdt,hdn->htn", q, k) * SCALE + f64(mask)[None]
    e = np.exp(sc - sc.max(axis=2, keepdims=True))
    p = e / e.sum(axis=2, keepdims=True)
    vv = f64(v).reshape(N, H, D)
    return np.einsum("htn,nhd->hdt", p, vv).reshape(C, T)

@@ -1,0 +1,125 @@
+import concourse.mybir as mybir
+from concourse.masks import make_identity
+
+H, D, HALF, S, N, T = 8, 128, 64, 256, 128, 128
+SCALE = D ** -0.5
+FLOPS = 2 * 2 * H * T * N * D
+
+BF16, F32, U16 = mybir.dt.bfloat16, mybir.dt.float32, mybir.dt.uint16
+MULT, ADD = mybir.AluOpType.mult, mybir.AluOpType.add
+EXP, COPY = mybir.ActivationFunctionType.Exp, mybir.ActivationFunctionType.Copy
+ROW = mybir.AxisListType.X
+
+
+def tile_crossattention_kernel(tc, kstore, x, v, cos, sin, mask, offs, out):
+    nc = tc.nc
+    with (
+        tc.tile_pool(name="held", bufs=1) as held,
+        tc.tile_pool(name="heads", bufs=H) as heads,
+        tc.psum_pool(name="score_banks", bufs=3) as score_banks,
+        tc.psum_pool(name="flip_banks", bufs=2) as flip_banks,
+        tc.psum_pool(name="out_banks", bufs=3) as out_banks,
+    ):
+        offsets = held.tile([128, N // 16], U16, name="offsets")
+        nc.sync.dma_start(offsets[:], offs)
+
+        cos_bf = held.tile([D, N], BF16, name="cos_bf")
+        sin_bf = held.tile([D, N], BF16, name="sin_bf")
+        for half in range(2):
+            rows = slice(half * HALF, (half + 1) * HALF)
+            nc.scalar.dma_start(cos_bf[rows, :], cos)
+            nc.scalar.dma_start(sin_bf[rows, :], sin)
+        mask_sb = held.tile([T, N], F32, name="mask_sb")
+        nc.scalar.dma_start(mask_sb[:], mask)
+        v_sb = held.tile([N, H * D], BF16, name="v_sb")
+        nc.scalar.dma_start(v_sb[:], v)
+
+        ks_halves = kstore.rearrange("(h two d) s -> two d h s", two=2, d=HALF)
+        x_halves = x.rearrange("(h two d) t -> two d h t", two=2, d=HALF)
+        ks_plain, ks_turned = [], []
+
+        def load_pair(pair):
+            two_heads = slice(2 * pair, 2 * pair + 2)
+            plain = held.tile([D, 2, S], BF16, name=f"ks_plain{pair}")
+            turned = held.tile([D, 2, S], BF16, name=f"ks_turned{pair}")
+            nc.sync.dma_start(plain[:], kstore.rearrange("(h d) s -> d h s", d=D)[:, two_heads, :])
+            nc.sync.dma_start(turned[0:HALF], ks_halves[1][:, two_heads, :])
+            nc.sync.dma_start(turned[HALF:D], ks_halves[0][:, two_heads, :])
+            ks_plain.append(plain)
+            ks_turned.append(turned)
+
+        load_pair(0)
+        x_plain = held.tile([D, H, T], BF16, name="x_plain")
+        x_turned = held.tile([D, H, T], BF16, name="x_turned")
+        nc.sync.dma_start(x_plain[:], x.rearrange("(h d) t -> d h t", d=D))
+        nc.sync.dma_start(x_turned[0:HALF], x_halves[1])
+        nc.sync.dma_start(x_turned[HALF:D], x_halves[0])
+        for pair in range(1, H // 2):
+            load_pair(pair)
+
+        warm = held.tile([128, 1], F32, name="warm")
+        nc.vector.memset(warm[:], 0.0)
+        nc.scalar.activation(warm[:], warm[:], EXP)
+
+        ident_bf = held.tile([128, 128], BF16, name="ident_bf")
+        make_identity(nc, ident_bf[:])
+        ident_f32 = held.tile([128, 128], F32, name="ident_f32")
+        make_identity(nc, ident_f32[:])
+
+        cos2 = held.tile([D, N], F32, name="cos2")
+        nc.scalar.copy(cos2[:], cos_bf[:])
+        sin2 = held.tile([D, N], F32, name="sin2")
+        nc.scalar.mul(sin2[0:HALF], sin_bf[0:HALF], -1.0)
+        nc.scalar.copy(sin2[HALF:D], sin_bf[HALF:D])
+        mask_up = held.tile([T, N], F32, name="mask_up")
+        nc.scalar.mul(mask_up[:], mask_sb[:], 1.0 / SCALE)
+
+        neg_max = held.tile([T, H], F32, name="neg_max")
+        shift = held.tile([T, H], F32, name="shift")
+        total = held.tile([T, H], F32, name="total")
+        inv_total = held.tile([T, H], F32, name="inv_total")
+
+        for h in range(H):
+            pair, member = divmod(h, 2)
+            col = slice(h, h + 1)
+
+            q_cos = heads.tile([D, T], F32, name="q_cos")
+            q_sin = heads.tile([D, T], F32, name="q_sin")
+            q = heads.tile([D, T], BF16, name="q")
+            nc.vector.tensor_tensor(q_cos[:], x_plain[:, h, :], cos2[:], MULT)
+            nc.vector.tensor_tensor(q_sin[:], x_turned[:, h, :], sin2[:], MULT)
+            nc.vector.tensor_tensor(q[:], q_cos[:], q_sin[:], ADD)
+
+            win_plain = heads.tile([D, S], F32, name="win_plain")
+            win_turned = heads.tile([D, S], F32, name="win_turned")
+            nc.scalar.copy(win_plain[:], ks_plain[pair][:, member, :])
+            nc.scalar.copy(win_turned[:], ks_turned[pair][:, member, :])
+
+            k_cos = heads.tile([D, N], F32, name="k_cos")
+            k_sin = heads.tile([D, N], F32, name="k_sin")
+            k = heads.tile([D, N], BF16, name="k")
+            nc.vector.tensor_tensor(k_cos[:], win_plain[:].indirect(offsets[:]), cos2[:], MULT)
+            nc.vector.tensor_tensor(k_sin[:], win_turned[:].indirect(offsets[:]), sin2[:], MULT)
+            nc.vector.tensor_tensor(k[:], k_cos[:], k_sin[:], ADD)
+
+            scores = score_banks.tile([T, N], F32, name="scores")
+            nc.tensor.matmul(scores[:], ident_f32[:], mask_up[:], start=True, stop=False)
+            nc.tensor.matmul(scores[:], q[:], k[:], start=False, stop=True)
+
+            nc.vector.reduce_max(neg_max[:, col], scores[:], ROW, negate=True)
+            nc.scalar.mul(shift[:, col], neg_max[:, col], SCALE)
+            e = heads.tile([T, N], F32, name="e")
+            nc.scalar.activation(e[:], scores[:], EXP, bias=shift[:, col], scale=SCALE, accum_out=total[:, col])
+            nc.vector.reciprocal(inv_total[:, col], total[:, col])
+            p = heads.tile([T, N], BF16, name="p")
+            nc.scalar.activation(p[:], e[:], COPY, scale=inv_total[:, col])
+
+            flipped = flip_banks.tile([N, T], BF16, name="flipped")
+            nc.tensor.transpose(flipped[:], p[:], ident_bf[:])
+            p_flipped = heads.tile([N, T], BF16, name="p_flipped")
+            nc.scalar.copy(p_flipped[:], flipped[:])
+            product = out_banks.tile([D, T], F32, name="product")
+            nc.tensor.matmul(product[:], v_sb[:, h * D : (h + 1) * D], p_flipped[:], start=True, stop=True)
+            result = heads.tile([D, T], F32, name="result")
+            nc.scalar.copy(result[:], product[:])
+            nc.sync.dma_start(out[h * D : (h + 1) * D, :], result[:])

@@ -4,6 +4,7 @@ from concourse.masks import make_identity
 H, D, HALF, S, N, T = 8, 128, 64, 256, 128, 128
 SCALE = D ** -0.5
 FLOPS = 2 * 2 * H * T * N * D
+PAIR = 2
 
 BF16, F32, U16 = mybir.dt.bfloat16, mybir.dt.float32, mybir.dt.uint16
 MULT, ADD = mybir.AluOpType.mult, mybir.AluOpType.add
@@ -16,61 +17,52 @@ def tile_crossattention_kernel(tc, kstore, x, v, cos, sin, mask, offs, out):
     with (
         tc.tile_pool(name="held", bufs=1) as held,
         tc.tile_pool(name="heads", bufs=H) as heads,
-        tc.psum_pool(name="score_banks", bufs=3) as score_banks,
-        tc.psum_pool(name="flip_banks", bufs=2) as flip_banks,
-        tc.psum_pool(name="out_banks", bufs=3) as out_banks,
+        tc.psum_pool(name="turned_banks", bufs=2) as turned_banks,
+        tc.psum_pool(name="key_banks", bufs=2) as key_banks,
+        tc.psum_pool(name="score_banks", bufs=2) as score_banks,
+        tc.psum_pool(name="flip_banks", bufs=1) as flip_banks,
+        tc.psum_pool(name="out_banks", bufs=1) as out_banks,
     ):
         offsets = held.tile([128, N // 16], U16, name="offsets")
         nc.sync.dma_start(offsets[:], offs)
-
         cos_bf = held.tile([D, N], BF16, name="cos_bf")
         sin_bf = held.tile([D, N], BF16, name="sin_bf")
         for half in range(2):
             rows = slice(half * HALF, (half + 1) * HALF)
-            nc.scalar.dma_start(cos_bf[rows, :], cos)
-            nc.scalar.dma_start(sin_bf[rows, :], sin)
+            nc.sync.dma_start(cos_bf[rows, :], cos)
+            nc.sync.dma_start(sin_bf[rows, :], sin)
         mask_sb = held.tile([T, N], F32, name="mask_sb")
-        nc.scalar.dma_start(mask_sb[:], mask)
+        nc.sync.dma_start(mask_sb[:], mask)
+        x_bf, ks_bf = [], []
+        for pair in range(H // PAIR):
+            these = slice(pair * PAIR, (pair + 1) * PAIR)
+            x_pair = held.tile([D, PAIR, T], BF16, name=f"x_bf{pair}")
+            nc.sync.dma_start(x_pair[:], x.rearrange("(h d) t -> d h t", d=D)[:, these, :])
+            x_bf.append(x_pair)
+            ks_pair = held.tile([D, PAIR, S], BF16, name=f"ks_bf{pair}")
+            nc.sync.dma_start(ks_pair[:], kstore.rearrange("(h d) s -> d h s", d=D)[:, these, :])
+            ks_bf.append(ks_pair)
         v_sb = held.tile([N, H * D], BF16, name="v_sb")
-        nc.scalar.dma_start(v_sb[:], v)
-
-        ks_halves = kstore.rearrange("(h two d) s -> two d h s", two=2, d=HALF)
-        x_halves = x.rearrange("(h two d) t -> two d h t", two=2, d=HALF)
-        ks_plain, ks_turned = [], []
-
-        def load_pair(pair):
-            two_heads = slice(2 * pair, 2 * pair + 2)
-            plain = held.tile([D, 2, S], BF16, name=f"ks_plain{pair}")
-            turned = held.tile([D, 2, S], BF16, name=f"ks_turned{pair}")
-            nc.sync.dma_start(plain[:], kstore.rearrange("(h d) s -> d h s", d=D)[:, two_heads, :])
-            nc.sync.dma_start(turned[0:HALF], ks_halves[1][:, two_heads, :])
-            nc.sync.dma_start(turned[HALF:D], ks_halves[0][:, two_heads, :])
-            ks_plain.append(plain)
-            ks_turned.append(turned)
-
-        load_pair(0)
-        x_plain = held.tile([D, H, T], BF16, name="x_plain")
-        x_turned = held.tile([D, H, T], BF16, name="x_turned")
-        nc.sync.dma_start(x_plain[:], x.rearrange("(h d) t -> d h t", d=D))
-        nc.sync.dma_start(x_turned[0:HALF], x_halves[1])
-        nc.sync.dma_start(x_turned[HALF:D], x_halves[0])
-        for pair in range(1, H // 2):
-            load_pair(pair)
+        nc.sync.dma_start(v_sb[:], v)
 
         warm = held.tile([128, 1], F32, name="warm")
         nc.vector.memset(warm[:], 0.0)
         nc.scalar.activation(warm[:], warm[:], EXP)
 
-        ident_bf = held.tile([128, 128], BF16, name="ident_bf")
-        make_identity(nc, ident_bf[:])
         ident_f32 = held.tile([128, 128], F32, name="ident_f32")
         make_identity(nc, ident_f32[:])
+        turn_f32 = held.tile([128, 128], F32, name="turn_f32")
+        nc.gpsimd.tensor_scalar_mul(turn_f32[:, 0:HALF], ident_f32[:, HALF:D], -1.0)
+        nc.gpsimd.tensor_copy(turn_f32[:, HALF:D], ident_f32[:, 0:HALF])
+        turn_bf = held.tile([128, 128], BF16, name="turn_bf")
+        nc.gpsimd.tensor_copy(turn_bf[:], turn_f32[:])
+        ident_bf = held.tile([128, 128], BF16, name="ident_bf")
+        nc.gpsimd.tensor_copy(ident_bf[:], ident_f32[:])
 
         cos2 = held.tile([D, N], F32, name="cos2")
         nc.scalar.copy(cos2[:], cos_bf[:])
         sin2 = held.tile([D, N], F32, name="sin2")
-        nc.scalar.mul(sin2[0:HALF], sin_bf[0:HALF], -1.0)
-        nc.scalar.copy(sin2[HALF:D], sin_bf[HALF:D])
+        nc.scalar.copy(sin2[:], sin_bf[:])
         mask_up = held.tile([T, N], F32, name="mask_up")
         nc.scalar.mul(mask_up[:], mask_sb[:], 1.0 / SCALE)
 
@@ -79,28 +71,46 @@ def tile_crossattention_kernel(tc, kstore, x, v, cos, sin, mask, offs, out):
         total = held.tile([T, H], F32, name="total")
         inv_total = held.tile([T, H], F32, name="inv_total")
 
-        for h in range(H):
-            pair, member = divmod(h, 2)
-            col = slice(h, h + 1)
+        def make_keys(h):
+            pair, member = divmod(h, PAIR)
+            window = heads.tile([D, S], F32, name="window")
+            nc.scalar.copy(window[:], ks_bf[pair][:, member, :])
+            k_cos = heads.tile([D, N], F32, name="k_cos")
+            k_sin = heads.tile([D, N], F32, name="k_sin")
+            nc.vector.tensor_tensor(k_cos[:], window[:].indirect(offsets[:]), cos2[:], MULT)
+            nc.vector.tensor_tensor(k_sin[:], window[:].indirect(offsets[:]), sin2[:], MULT)
+            k_sum = key_banks.tile([D, N], F32, name="k_sum")
+            nc.tensor.matmul(k_sum[:], ident_f32[:], k_cos[:], start=True, stop=False)
+            nc.tensor.matmul(k_sum[:], turn_f32[:], k_sin[:], start=False, stop=True)
+            k = heads.tile([D, N], BF16, name="k")
+            nc.scalar.copy(k[:], k_sum[:])
+            return k
 
+        def turn_x(pair):
+            x_turned = turned_banks.tile([D, PAIR, T], F32, name="x_turned")
+            nc.tensor.matmul(x_turned[:], turn_bf[:], x_bf[pair][:], start=True, stop=True)
+            return x_turned
+
+        def make_queries(h, x_turned):
+            pair, member = divmod(h, PAIR)
             q_cos = heads.tile([D, T], F32, name="q_cos")
             q_sin = heads.tile([D, T], F32, name="q_sin")
             q = heads.tile([D, T], BF16, name="q")
-            nc.vector.tensor_tensor(q_cos[:], x_plain[:, h, :], cos2[:], MULT)
-            nc.vector.tensor_tensor(q_sin[:], x_turned[:, h, :], sin2[:], MULT)
+            nc.vector.tensor_tensor(q_cos[:], x_bf[pair][:, member, :], cos2[:], MULT)
+            nc.vector.tensor_tensor(q_sin[:], x_turned[:, member, :], sin2[:], MULT)
             nc.vector.tensor_tensor(q[:], q_cos[:], q_sin[:], ADD)
+            return q
 
-            win_plain = heads.tile([D, S], F32, name="win_plain")
-            win_turned = heads.tile([D, S], F32, name="win_turned")
-            nc.scalar.copy(win_plain[:], ks_plain[pair][:, member, :])
-            nc.scalar.copy(win_turned[:], ks_turned[pair][:, member, :])
-
-            k_cos = heads.tile([D, N], F32, name="k_cos")
-            k_sin = heads.tile([D, N], F32, name="k_sin")
-            k = heads.tile([D, N], BF16, name="k")
-            nc.vector.tensor_tensor(k_cos[:], win_plain[:].indirect(offsets[:]), cos2[:], MULT)
-            nc.vector.tensor_tensor(k_sin[:], win_turned[:].indirect(offsets[:]), sin2[:], MULT)
-            nc.vector.tensor_tensor(k[:], k_cos[:], k_sin[:], ADD)
+        k_next = make_keys(0)
+        x_turned = None
+        for h in range(H):
+            col = slice(h, h + 1)
+            k = k_next
+            if h + 1 < H:
+                k_next = make_keys(h + 1)
+            if h % PAIR == 0:
+                x_turned = turn_x(h // PAIR)
+            q = make_queries(h, x_turned)
 
             scores = score_banks.tile([T, N], F32, name="scores")
             nc.tensor.matmul(scores[:], ident_f32[:], mask_up[:], start=True, stop=False)

@@ -4,6 +4,7 @@ from concourse.masks import make_identity
 H, D, HALF, S, N, T = 8, 128, 64, 256, 128, 128
 SCALE = D ** -0.5
 FLOPS = 2 * 2 * H * T * N * D
+GROUP = 4
 PAIR = 2
 
 BF16, F32, U16 = mybir.dt.bfloat16, mybir.dt.float32, mybir.dt.uint16
@@ -17,11 +18,10 @@ def tile_crossattention_kernel(tc, kstore, x, v, cos, sin, mask, offs, out):
     with (
         tc.tile_pool(name="held", bufs=1) as held,
         tc.tile_pool(name="heads", bufs=H) as heads,
-        tc.psum_pool(name="turned_banks", bufs=2) as turned_banks,
-        tc.psum_pool(name="key_banks", bufs=2) as key_banks,
-        tc.psum_pool(name="score_banks", bufs=2) as score_banks,
-        tc.psum_pool(name="flip_banks", bufs=1) as flip_banks,
-        tc.psum_pool(name="out_banks", bufs=1) as out_banks,
+        tc.psum_pool(name="turned_banks", bufs=1) as turned_banks,
+        tc.psum_pool(name="score_banks", bufs=3) as score_banks,
+        tc.psum_pool(name="flip_banks", bufs=2) as flip_banks,
+        tc.psum_pool(name="out_banks", bufs=2) as out_banks,
     ):
         offsets = held.tile([128, N // 16], U16, name="offsets")
         nc.sync.dma_start(offsets[:], offs)
@@ -31,17 +31,22 @@ def tile_crossattention_kernel(tc, kstore, x, v, cos, sin, mask, offs, out):
             rows = slice(half * HALF, (half + 1) * HALF)
             nc.sync.dma_start(cos_bf[rows, :], cos)
             nc.sync.dma_start(sin_bf[rows, :], sin)
+        x_plain = held.tile([D, H, T], BF16, name="x_plain")
+        nc.sync.dma_start(x_plain[:], x.rearrange("(h d) t -> d h t", d=D))
+        ks_halves = kstore.rearrange("(h two d) s -> two d h s", two=2, d=HALF)
+        ks_plain, ks_turned = [], []
         mask_sb = held.tile([T, N], F32, name="mask_sb")
-        nc.sync.dma_start(mask_sb[:], mask)
-        x_bf, ks_bf = [], []
-        for pair in range(H // PAIR):
-            these = slice(pair * PAIR, (pair + 1) * PAIR)
-            x_pair = held.tile([D, PAIR, T], BF16, name=f"x_bf{pair}")
-            nc.sync.dma_start(x_pair[:], x.rearrange("(h d) t -> d h t", d=D)[:, these, :])
-            x_bf.append(x_pair)
-            ks_pair = held.tile([D, PAIR, S], BF16, name=f"ks_bf{pair}")
-            nc.sync.dma_start(ks_pair[:], kstore.rearrange("(h d) s -> d h s", d=D)[:, these, :])
-            ks_bf.append(ks_pair)
+        for g in range(H // GROUP):
+            these = slice(g * GROUP, (g + 1) * GROUP)
+            plain = held.tile([D, GROUP, S], BF16, name=f"ks_plain{g}")
+            turned = held.tile([D, GROUP, S], BF16, name=f"ks_turned{g}")
+            nc.sync.dma_start(plain[:], kstore.rearrange("(h d) s -> d h s", d=D)[:, these, :])
+            nc.sync.dma_start(turned[0:HALF], ks_halves[1][:, these, :])
+            nc.sync.dma_start(turned[HALF:D], ks_halves[0][:, these, :])
+            ks_plain.append(plain)
+            ks_turned.append(turned)
+            if g == 0:
+                nc.sync.dma_start(mask_sb[:], mask)
         v_sb = held.tile([N, H * D], BF16, name="v_sb")
         nc.sync.dma_start(v_sb[:], v)
 
@@ -51,18 +56,17 @@ def tile_crossattention_kernel(tc, kstore, x, v, cos, sin, mask, offs, out):
 
         ident_f32 = held.tile([128, 128], F32, name="ident_f32")
         make_identity(nc, ident_f32[:])
-        turn_f32 = held.tile([128, 128], F32, name="turn_f32")
-        nc.gpsimd.tensor_scalar_mul(turn_f32[:, 0:HALF], ident_f32[:, HALF:D], -1.0)
-        nc.gpsimd.tensor_copy(turn_f32[:, HALF:D], ident_f32[:, 0:HALF])
         turn_bf = held.tile([128, 128], BF16, name="turn_bf")
-        nc.gpsimd.tensor_copy(turn_bf[:], turn_f32[:])
+        nc.gpsimd.tensor_copy(turn_bf[:, 0:HALF], ident_f32[:, HALF:D])
+        nc.gpsimd.tensor_copy(turn_bf[:, HALF:D], ident_f32[:, 0:HALF])
         ident_bf = held.tile([128, 128], BF16, name="ident_bf")
         nc.gpsimd.tensor_copy(ident_bf[:], ident_f32[:])
 
         cos2 = held.tile([D, N], F32, name="cos2")
         nc.scalar.copy(cos2[:], cos_bf[:])
         sin2 = held.tile([D, N], F32, name="sin2")
-        nc.scalar.copy(sin2[:], sin_bf[:])
+        nc.scalar.mul(sin2[0:HALF], sin_bf[0:HALF], -1.0)
+        nc.scalar.copy(sin2[HALF:D], sin_bf[HALF:D])
         mask_up = held.tile([T, N], F32, name="mask_up")
         nc.scalar.mul(mask_up[:], mask_sb[:], 1.0 / SCALE)
 
@@ -72,44 +76,35 @@ def tile_crossattention_kernel(tc, kstore, x, v, cos, sin, mask, offs, out):
         inv_total = held.tile([T, H], F32, name="inv_total")
 
         def make_keys(h):
-            pair, member = divmod(h, PAIR)
-            window = heads.tile([D, S], F32, name="window")
-            nc.scalar.copy(window[:], ks_bf[pair][:, member, :])
+            g, member = divmod(h, GROUP)
+            win_plain = heads.tile([D, S], F32, name="win_plain")
+            win_turned = heads.tile([D, S], F32, name="win_turned")
+            nc.scalar.copy(win_plain[:], ks_plain[g][:, member, :])
+            nc.scalar.copy(win_turned[:], ks_turned[g][:, member, :])
             k_cos = heads.tile([D, N], F32, name="k_cos")
             k_sin = heads.tile([D, N], F32, name="k_sin")
-            nc.vector.tensor_tensor(k_cos[:], window[:].indirect(offsets[:]), cos2[:], MULT)
-            nc.vector.tensor_tensor(k_sin[:], window[:].indirect(offsets[:]), sin2[:], MULT)
-            k_sum = key_banks.tile([D, N], F32, name="k_sum")
-            nc.tensor.matmul(k_sum[:], ident_f32[:], k_cos[:], start=True, stop=False)
-            nc.tensor.matmul(k_sum[:], turn_f32[:], k_sin[:], start=False, stop=True)
             k = heads.tile([D, N], BF16, name="k")
-            nc.scalar.copy(k[:], k_sum[:])
+            nc.vector.tensor_tensor(k_cos[:], win_plain[:].indirect(offsets[:]), cos2[:], MULT)
+            nc.vector.tensor_tensor(k_sin[:], win_turned[:].indirect(offsets[:]), sin2[:], MULT)
+            nc.vector.tensor_tensor(k[:], k_cos[:], k_sin[:], ADD)
             return k
 
-        def turn_x(pair):
-            x_turned = turned_banks.tile([D, PAIR, T], F32, name="x_turned")
-            nc.tensor.matmul(x_turned[:], turn_bf[:], x_bf[pair][:], start=True, stop=True)
-            return x_turned
-
         def make_queries(h, x_turned):
-            pair, member = divmod(h, PAIR)
             q_cos = heads.tile([D, T], F32, name="q_cos")
             q_sin = heads.tile([D, T], F32, name="q_sin")
             q = heads.tile([D, T], BF16, name="q")
-            nc.vector.tensor_tensor(q_cos[:], x_bf[pair][:, member, :], cos2[:], MULT)
-            nc.vector.tensor_tensor(q_sin[:], x_turned[:, member, :], sin2[:], MULT)
+            nc.vector.tensor_tensor(q_cos[:], x_plain[:, h, :], cos2[:], MULT)
+            nc.vector.tensor_tensor(q_sin[:], x_turned[:, h % PAIR, :], sin2[:], MULT)
             nc.vector.tensor_tensor(q[:], q_cos[:], q_sin[:], ADD)
             return q
 
-        k_next = make_keys(0)
         x_turned = None
         for h in range(H):
             col = slice(h, h + 1)
-            k = k_next
-            if h + 1 < H:
-                k_next = make_keys(h + 1)
+            k = make_keys(h)
             if h % PAIR == 0:
-                x_turned = turn_x(h // PAIR)
+                x_turned = turned_banks.tile([D, PAIR, T], F32, name="x_turned")
+                nc.tensor.matmul(x_turned[:], turn_bf[:], x_plain[:, h : h + PAIR, :], start=True, stop=True)
             q = make_queries(h, x_turned)
 
             scores = score_banks.tile([T, N], F32, name="scores")

@@ -5,7 +5,6 @@ H, D, HALF, S, N, T = 8, 128, 64, 256, 128, 128
 SCALE = D ** -0.5
 FLOPS = 2 * 2 * H * T * N * D
 GROUP = 4
-PAIR = 2
 
 BF16, F32, U16 = mybir.dt.bfloat16, mybir.dt.float32, mybir.dt.uint16
 MULT, ADD = mybir.AluOpType.mult, mybir.AluOpType.add
@@ -23,30 +22,37 @@ def tile_crossattention_kernel(tc, kstore, x, v, cos, sin, mask, offs, out):
         tc.psum_pool(name="flip_banks", bufs=2) as flip_banks,
         tc.psum_pool(name="out_banks", bufs=2) as out_banks,
     ):
-        offsets = held.tile([128, N // 16], U16, name="offsets")
-        nc.sync.dma_start(offsets[:], offs)
-        cos_bf = held.tile([D, N], BF16, name="cos_bf")
-        sin_bf = held.tile([D, N], BF16, name="sin_bf")
-        for half in range(2):
-            rows = slice(half * HALF, (half + 1) * HALF)
-            nc.sync.dma_start(cos_bf[rows, :], cos)
-            nc.sync.dma_start(sin_bf[rows, :], sin)
-        x_plain = held.tile([D, H, T], BF16, name="x_plain")
-        nc.sync.dma_start(x_plain[:], x.rearrange("(h d) t -> d h t", d=D))
-        ks_halves = kstore.rearrange("(h two d) s -> two d h s", two=2, d=HALF)
-        ks_plain, ks_turned = [], []
-        mask_sb = held.tile([T, N], F32, name="mask_sb")
-        for g in range(H // GROUP):
+        def load_twice(table, name):
+            twice = held.tile([D, N], BF16, name=name)
+            nc.sync.dma_start(twice[0:HALF, :], table)
+            nc.sync.dma_start(twice[HALF:D, :], table)
+            return twice
+
+        def load_x(g):
+            x_group = held.tile([D, GROUP, T], BF16, name=f"x_plain{g}")
+            nc.sync.dma_start(x_group[:], x.rearrange("(h d) t -> d h t", d=D)[:, g * GROUP : (g + 1) * GROUP, :])
+            return x_group
+
+        def load_ks(g):
             these = slice(g * GROUP, (g + 1) * GROUP)
+            halves = kstore.rearrange("(h two d) s -> two d h s", two=2, d=HALF)
             plain = held.tile([D, GROUP, S], BF16, name=f"ks_plain{g}")
             turned = held.tile([D, GROUP, S], BF16, name=f"ks_turned{g}")
             nc.sync.dma_start(plain[:], kstore.rearrange("(h d) s -> d h s", d=D)[:, these, :])
-            nc.sync.dma_start(turned[0:HALF], ks_halves[1][:, these, :])
-            nc.sync.dma_start(turned[HALF:D], ks_halves[0][:, these, :])
-            ks_plain.append(plain)
-            ks_turned.append(turned)
-            if g == 0:
-                nc.sync.dma_start(mask_sb[:], mask)
+            nc.sync.dma_start(turned[0:HALF], halves[1][:, these, :])
+            nc.sync.dma_start(turned[HALF:D], halves[0][:, these, :])
+            return plain, turned
+
+        cos_bf = load_twice(cos, "cos_bf")
+        x_plain = [load_x(0)]
+        sin_bf = load_twice(sin, "sin_bf")
+        offsets = held.tile([128, N // 16], U16, name="offsets")
+        nc.sync.dma_start(offsets[:], offs)
+        ks_groups = [load_ks(0)]
+        x_plain.append(load_x(1))
+        mask_sb = held.tile([T, N], F32, name="mask_sb")
+        nc.sync.dma_start(mask_sb[:], mask)
+        ks_groups.append(load_ks(1))
         v_sb = held.tile([N, H * D], BF16, name="v_sb")
         nc.sync.dma_start(v_sb[:], v)
 
@@ -75,12 +81,25 @@ def tile_crossattention_kernel(tc, kstore, x, v, cos, sin, mask, offs, out):
         total = held.tile([T, H], F32, name="total")
         inv_total = held.tile([T, H], F32, name="inv_total")
 
+        def make_queries(g):
+            for_each_head = [D, GROUP, T]
+            x_turned = turned_banks.tile(for_each_head, F32, name="x_turned")
+            nc.tensor.matmul(x_turned[:], turn_bf[:], x_plain[g][:], start=True, stop=True)
+            q_cos = held.tile(for_each_head, F32, name=f"q_cos{g}")
+            q_sin = held.tile(for_each_head, F32, name=f"q_sin{g}")
+            q = held.tile(for_each_head, BF16, name=f"q{g}")
+            nc.vector.tensor_tensor(q_cos[:], x_plain[g][:], cos2[:].unsqueeze(1).to_broadcast(for_each_head), MULT)
+            nc.vector.tensor_tensor(q_sin[:], x_turned[:], sin2[:].unsqueeze(1).to_broadcast(for_each_head), MULT)
+            nc.vector.tensor_tensor(q[:], q_cos[:], q_sin[:], ADD)
+            return q
+
         def make_keys(h):
             g, member = divmod(h, GROUP)
+            ks_plain, ks_turned = ks_groups[g]
             win_plain = heads.tile([D, S], F32, name="win_plain")
             win_turned = heads.tile([D, S], F32, name="win_turned")
-            nc.scalar.copy(win_plain[:], ks_plain[g][:, member, :])
-            nc.scalar.copy(win_turned[:], ks_turned[g][:, member, :])
+            nc.scalar.copy(win_plain[:], ks_plain[:, member, :])
+            nc.scalar.copy(win_turned[:], ks_turned[:, member, :])
             k_cos = heads.tile([D, N], F32, name="k_cos")
             k_sin = heads.tile([D, N], F32, name="k_sin")
             k = heads.tile([D, N], BF16, name="k")
@@ -89,27 +108,16 @@ def tile_crossattention_kernel(tc, kstore, x, v, cos, sin, mask, offs, out):
             nc.vector.tensor_tensor(k[:], k_cos[:], k_sin[:], ADD)
             return k
 
-        def make_queries(h, x_turned):
-            q_cos = heads.tile([D, T], F32, name="q_cos")
-            q_sin = heads.tile([D, T], F32, name="q_sin")
-            q = heads.tile([D, T], BF16, name="q")
-            nc.vector.tensor_tensor(q_cos[:], x_plain[:, h, :], cos2[:], MULT)
-            nc.vector.tensor_tensor(q_sin[:], x_turned[:, h % PAIR, :], sin2[:], MULT)
-            nc.vector.tensor_tensor(q[:], q_cos[:], q_sin[:], ADD)
-            return q
-
-        x_turned = None
+        q_group = None
         for h in range(H):
             col = slice(h, h + 1)
+            if h % GROUP == 0:
+                q_group = make_queries(h // GROUP)
             k = make_keys(h)
-            if h % PAIR == 0:
-                x_turned = turned_banks.tile([D, PAIR, T], F32, name="x_turned")
-                nc.tensor.matmul(x_turned[:], turn_bf[:], x_plain[:, h : h + PAIR, :], start=True, stop=True)
-            q = make_queries(h, x_turned)
 
             scores = score_banks.tile([T, N], F32, name="scores")
             nc.tensor.matmul(scores[:], ident_f32[:], mask_up[:], start=True, stop=False)
-            nc.tensor.matmul(scores[:], q[:], k[:], start=False, stop=True)
+            nc.tensor.matmul(scores[:], q_group[:, h % GROUP, :], k[:], start=False, stop=True)
 
             nc.vector.reduce_max(neg_max[:, col], scores[:], ROW, negate=True)
             nc.scalar.mul(shift[:, col], neg_max[:, col], SCALE)

@@ -130,7 +130,7 @@ def tile_crossattention_kernel(tc, kstore, x, v, cos, sin, mask, offs, out):
             flipped = flip_banks.tile([N, T], BF16, name="flipped")
             nc.tensor.transpose(flipped[:], p[:], ident_bf[:])
             p_flipped = heads.tile([N, T], BF16, name="p_flipped")
-            nc.scalar.copy(p_flipped[:], flipped[:])
+            nc.vector.tensor_copy(p_flipped[:], flipped[:])
             product = out_banks.tile([D, T], F32, name="product")
             nc.tensor.matmul(product[:], v_sb[:, h * D : (h + 1) * D], p_flipped[:], start=True, stop=True)
             result = heads.tile([D, T], F32, name="result")

@@ -7,9 +7,8 @@ FLOPS = 2 * 2 * H * T * N * D
 GROUP = 4
 
 BF16, F32, U16 = mybir.dt.bfloat16, mybir.dt.float32, mybir.dt.uint16
-MULT, ADD = mybir.AluOpType.mult, mybir.AluOpType.add
+MULT, ADD, MIN = mybir.AluOpType.mult, mybir.AluOpType.add, mybir.AluOpType.min
 EXP, COPY = mybir.ActivationFunctionType.Exp, mybir.ActivationFunctionType.Copy
-ROW = mybir.AxisListType.X
 
 
 def tile_crossattention_kernel(tc, kstore, x, v, cos, sin, mask, offs, out):
@@ -76,7 +75,6 @@ def tile_crossattention_kernel(tc, kstore, x, v, cos, sin, mask, offs, out):
         mask_up = held.tile([T, N], F32, name="mask_up")
         nc.scalar.mul(mask_up[:], mask_sb[:], 1.0 / SCALE)
 
-        neg_max = held.tile([T, H], F32, name="neg_max")
         shift = held.tile([T, H], F32, name="shift")
         total = held.tile([T, H], F32, name="total")
         inv_total = held.tile([T, H], F32, name="inv_total")
@@ -119,8 +117,8 @@ def tile_crossattention_kernel(tc, kstore, x, v, cos, sin, mask, offs, out):
             nc.tensor.matmul(scores[:], ident_f32[:], mask_up[:], start=True, stop=False)
             nc.tensor.matmul(scores[:], q_group[:, h % GROUP, :], k[:], start=False, stop=True)
 
-            nc.vector.reduce_max(neg_max[:, col], scores[:], ROW, negate=True)
-            nc.scalar.mul(shift[:, col], neg_max[:, col], SCALE)
+            negated = heads.tile([T, N], F32, name="negated")
+            nc.vector.tensor_scalar(negated[:], scores[:], -SCALE, None, MULT, MIN, accum_out=shift[:, col])
             e = heads.tile([T, N], F32, name="e")
             nc.scalar.activation(e[:], scores[:], EXP, bias=shift[:, col], scale=SCALE, accum_out=total[:, col])
             nc.vector.reciprocal(inv_total[:, col], total[:, col])

@@ -126,7 +126,7 @@ def tile_crossattention_kernel(tc, kstore, x, v, cos, sin, mask, offs, out):
             nc.scalar.activation(p[:], e[:], COPY, scale=inv_total[:, col])
 
             flipped = flip_banks.tile([N, T], BF16, name="flipped")
-            nc.tensor.transpose(flipped[:], p[:], ident_bf[:])
+            nc.tensor.matmul(flipped[:], p[:], ident_bf[:], start=True, stop=True)
             p_flipped = heads.tile([N, T], BF16, name="p_flipped")
             nc.vector.tensor_copy(p_flipped[:], flipped[:])
             product = out_banks.tile([D, T], F32, name="product")

import concourse.mybir as mybir
from concourse.masks import make_identity

H, D, HALF, S, N, T = 8, 128, 64, 256, 128, 128
SCALE = D ** -0.5
FLOPS = 2 * 2 * H * T * N * D
GROUP = 4

BF16, F32, U16 = mybir.dt.bfloat16, mybir.dt.float32, mybir.dt.uint16
MULT, ADD, MIN = mybir.AluOpType.mult, mybir.AluOpType.add, mybir.AluOpType.min
EXP, COPY = mybir.ActivationFunctionType.Exp, mybir.ActivationFunctionType.Copy


def tile_crossattention_kernel(tc, kstore, x, v, cos, sin, mask, offs, out):
    nc = tc.nc
    with (
        tc.tile_pool(name="held", bufs=1) as held,
        tc.tile_pool(name="heads", bufs=H) as heads,
        tc.psum_pool(name="turned_banks", bufs=1) as turned_banks,
        tc.psum_pool(name="score_banks", bufs=3) as score_banks,
        tc.psum_pool(name="flip_banks", bufs=2) as flip_banks,
        tc.psum_pool(name="out_banks", bufs=2) as out_banks,
    ):
        def load_twice(table, name):
            twice = held.tile([D, N], BF16, name=name)
            nc.sync.dma_start(twice[0:HALF, :], table)
            nc.sync.dma_start(twice[HALF:D, :], table)
            return twice

        def load_x(g):
            x_group = held.tile([D, GROUP, T], BF16, name=f"x_plain{g}")
            nc.sync.dma_start(x_group[:], x.rearrange("(h d) t -> d h t", d=D)[:, g * GROUP : (g + 1) * GROUP, :])
            return x_group

        def load_ks(g):
            these = slice(g * GROUP, (g + 1) * GROUP)
            halves = kstore.rearrange("(h two d) s -> two d h s", two=2, d=HALF)
            plain = held.tile([D, GROUP, S], BF16, name=f"ks_plain{g}")
            turned = held.tile([D, GROUP, S], BF16, name=f"ks_turned{g}")
            nc.sync.dma_start(plain[:], kstore.rearrange("(h d) s -> d h s", d=D)[:, these, :])
            nc.sync.dma_start(turned[0:HALF], halves[1][:, these, :])
            nc.sync.dma_start(turned[HALF:D], halves[0][:, these, :])
            return plain, turned

        cos_bf = load_twice(cos, "cos_bf")
        x_plain = [load_x(0)]
        sin_bf = load_twice(sin, "sin_bf")
        offsets = held.tile([128, N // 16], U16, name="offsets")
        nc.sync.dma_start(offsets[:], offs)
        ks_groups = [load_ks(0)]
        x_plain.append(load_x(1))
        mask_sb = held.tile([T, N], F32, name="mask_sb")
        nc.sync.dma_start(mask_sb[:], mask)
        ks_groups.append(load_ks(1))
        v_sb = held.tile([N, H * D], BF16, name="v_sb")
        nc.sync.dma_start(v_sb[:], v)

        warm = held.tile([128, 1], F32, name="warm")
        nc.vector.memset(warm[:], 0.0)
        nc.scalar.activation(warm[:], warm[:], EXP)

        ident_f32 = held.tile([128, 128], F32, name="ident_f32")
        make_identity(nc, ident_f32[:])
        turn_bf = held.tile([128, 128], BF16, name="turn_bf")
        nc.gpsimd.tensor_copy(turn_bf[:, 0:HALF], ident_f32[:, HALF:D])
        nc.gpsimd.tensor_copy(turn_bf[:, HALF:D], ident_f32[:, 0:HALF])
        ident_bf = held.tile([128, 128], BF16, name="ident_bf")
        nc.gpsimd.tensor_copy(ident_bf[:], ident_f32[:])

        cos2 = held.tile([D, N], F32, name="cos2")
        nc.scalar.copy(cos2[:], cos_bf[:])
        sin2 = held.tile([D, N], F32, name="sin2")
        nc.scalar.mul(sin2[0:HALF], sin_bf[0:HALF], -1.0)
        nc.scalar.copy(sin2[HALF:D], sin_bf[HALF:D])
        mask_up = held.tile([T, N], F32, name="mask_up")
        nc.scalar.mul(mask_up[:], mask_sb[:], 1.0 / SCALE)

        shift = held.tile([T, H], F32, name="shift")
        total = held.tile([T, H], F32, name="total")
        inv_total = held.tile([T, H], F32, name="inv_total")

        def make_queries(g):
            for_each_head = [D, GROUP, T]
            x_turned = turned_banks.tile(for_each_head, F32, name="x_turned")
            nc.tensor.matmul(x_turned[:], turn_bf[:], x_plain[g][:], start=True, stop=True)
            q_cos = held.tile(for_each_head, F32, name=f"q_cos{g}")
            q_sin = held.tile(for_each_head, F32, name=f"q_sin{g}")
            q = held.tile(for_each_head, BF16, name=f"q{g}")
            nc.vector.tensor_tensor(q_cos[:], x_plain[g][:], cos2[:].unsqueeze(1).to_broadcast(for_each_head), MULT)
            nc.vector.tensor_tensor(q_sin[:], x_turned[:], sin2[:].unsqueeze(1).to_broadcast(for_each_head), MULT)
            nc.vector.tensor_tensor(q[:], q_cos[:], q_sin[:], ADD)
            return q

        def make_keys(h):
            g, member = divmod(h, GROUP)
            ks_plain, ks_turned = ks_groups[g]
            win_plain = heads.tile([D, S], F32, name="win_plain")
            win_turned = heads.tile([D, S], F32, name="win_turned")
            nc.scalar.copy(win_plain[:], ks_plain[:, member, :])
            nc.scalar.copy(win_turned[:], ks_turned[:, member, :])
            k_cos = heads.tile([D, N], F32, name="k_cos")
            k_sin = heads.tile([D, N], F32, name="k_sin")
            k = heads.tile([D, N], BF16, name="k")
            nc.vector.tensor_tensor(k_cos[:], win_plain[:].indirect(offsets[:]), cos2[:], MULT)
            nc.vector.tensor_tensor(k_sin[:], win_turned[:].indirect(offsets[:]), sin2[:], MULT)
            nc.vector.tensor_tensor(k[:], k_cos[:], k_sin[:], ADD)
            return k

        q_group = None
        for h in range(H):
            col = slice(h, h + 1)
            if h % GROUP == 0:
                q_group = make_queries(h // GROUP)
            k = make_keys(h)

            scores = score_banks.tile([T, N], F32, name="scores")
            nc.tensor.matmul(scores[:], ident_f32[:], mask_up[:], start=True, stop=False)
            nc.tensor.matmul(scores[:], q_group[:, h % GROUP, :], k[:], start=False, stop=True)

            negated = heads.tile([T, N], F32, name="negated")
            nc.vector.tensor_scalar(negated[:], scores[:], -SCALE, None, MULT, MIN, accum_out=shift[:, col])
            e = heads.tile([T, N], F32, name="e")
            nc.scalar.activation(e[:], scores[:], EXP, bias=shift[:, col], scale=SCALE, accum_out=total[:, col])
            nc.vector.reciprocal(inv_total[:, col], total[:, col])
            p = heads.tile([T, N], BF16, name="p")
            nc.scalar.activation(p[:], e[:], COPY, scale=inv_total[:, col])

            flipped = flip_banks.tile([N, T], BF16, name="flipped")
            nc.tensor.matmul(flipped[:], p[:], ident_bf[:], start=True, stop=True)
            p_flipped = heads.tile([N, T], BF16, name="p_flipped")
            nc.vector.tensor_copy(p_flipped[:], flipped[:])
            product = out_banks.tile([D, T], F32, name="product")
            nc.tensor.matmul(product[:], v_sb[:, h * D : (h + 1) * D], p_flipped[:], start=True, stop=True)
            result = heads.tile([D, T], F32, name="result")
            nc.scalar.copy(result[:], product[:])
            nc.sync.dma_start(out[h * D : (h + 1) * D, :], result[:])
